import numpy as np
import ml_dtypes


def mxq(x, axis, fmt="e4m3"):
    dtype, down = {"e4m3": (ml_dtypes.float8_e4m3fn, 7), "e5m2": (ml_dtypes.float8_e5m2, 14)}[fmt]
    v = np.moveaxis(np.asarray(x, np.float32).astype(ml_dtypes.bfloat16).astype(np.float64), axis, -1)
    blocks = v.reshape(v.shape[:-1] + (-1, 32))
    amax = np.abs(blocks).max(-1, keepdims=True)
    byte = np.maximum(np.where(amax > 0, np.frexp(amax)[1] - 1 + 127, 0) - down, 1)
    scale = np.exp2(byte - 127.0)
    codes = (blocks / scale).astype(np.float32).astype(dtype).astype(np.float64)
    return np.moveaxis((codes * scale).reshape(v.shape), -1, axis)


WIDE = False


def mx_kscale(k):
    if not WIDE:
        return np.ones(k)
    levels = np.array([10, -10, 5, -5, 0])
    if k % 512:
        return np.exp2(np.random.permutation(np.resize(levels, k // 32))).repeat(32)
    a = np.empty((k // 512, 16))
    for p in range(k // 512):
        a[p, :8] = np.random.permutation(np.resize(levels, 8))
        for g in range(8):
            far = levels[np.abs(levels - a[p, g]) >= 10]
            a[p, g + 8] = far[np.random.randint(len(far))]
    return np.exp2(a.ravel()).repeat(32)


BF16 = ml_dtypes.bfloat16


def bf(x):
    return np.asarray(x, np.float32).astype(BF16)


def f64(x):
    return np.asarray(x).astype(np.float64)


E2M1 = np.array([0.0, 0.5, 1.0, 1.5, 2.0, 3.0, 4.0, 6.0, -0.0, -0.5, -1.0, -1.5, -2.0, -3.0, -4.0, -6.0])


def pack_weight(w, fmt):
    k, n = w.shape
    w = f64(bf(w)).reshape(k // 32, 32, n)
    amax = np.abs(w).max(1)
    if fmt == "e4m3":
        byte = np.frexp(amax)[1] - 1 + 127 - 7
    else:
        mant, ex = np.frexp(amax / 6.0)
        byte = np.where(mant > 0.5, ex, ex - 1) + 127
    byte = np.clip(np.where(amax > 0, byte, 1), 1, 254)
    scaled = (w * np.exp2(127.0 - byte)[:, None, :]).reshape(k, n).astype(np.float32)
    by_word = np.ascontiguousarray(scaled.reshape(k // 512, 128, 4, n).transpose(0, 1, 3, 2))
    if fmt == "e4m3":
        words = by_word.astype(ml_dtypes.float8_e4m3fn).view(np.uint8)
    else:
        c = by_word.astype(ml_dtypes.float4_e2m1fn).view(np.uint8) & 0xF
        words = c[..., 0::2] | (c[..., 1::2] << 4)
    return np.ascontiguousarray(words), np.ascontiguousarray(byte.astype(np.uint8).reshape(k // 512, 16, n))


def unpack_weight(words, scales, fmt):
    g, p, n, _ = words.shape
    if fmt == "e4m3":
        vals = np.ascontiguousarray(words).view(ml_dtypes.float8_e4m3fn).astype(np.float64)
    else:
        nib = np.empty((g, p, n, 4), np.uint8)
        nib[..., 0::2] = words & 0xF
        nib[..., 1::2] = words >> 4
        vals = E2M1[nib]
    vals = vals * np.repeat(np.exp2(scales.astype(np.float64) - 127.0), 8, axis=1)[..., None]
    return vals.transpose(0, 1, 3, 2).reshape(g * 512, n)
def pack4(w):
    words, scales = pack_weight(w, "e2m1")
    return words.reshape(words.shape[0], 128, -1), scales


def unpack4(words, scales):
    return unpack_weight(words.reshape(words.shape[0], 128, -1, 2), scales, "e2m1")


B, C, HH, WW, NH, HD, F = 4, 512, 16, 16, 8, 64, 2048
E = NH * HD


def draw0():
    s, t = mx_kscale(E), mx_kscale(C)
    o = bf(np.random.standard_normal((B, HH, WW, E)) * 0.6 * s)
    xn = bf(np.random.standard_normal((B, HH, WW, C)) * 0.5 * t)
    W_O_words, W_O_scales = pack4(np.random.standard_normal((E, C)) / np.sqrt(E) / s[:, None] * t)
    scale_attn = bf(0.5 * (1.0 + 0.1 * np.random.standard_normal(1)))
    ffn1_w_words, ffn1_w_scales = pack4((np.random.standard_normal((F, C)) * 3.0 / np.sqrt(C) / t).T)
    return {"o": o,
            "xn": xn,
            "W_O_words": W_O_words,
            "W_O_scales": W_O_scales,
            "scale_attn": scale_attn,
            "ffn1_w_words": ffn1_w_words,
            "ffn1_w_scales": ffn1_w_scales,
            "ffn1_b": bf(np.random.standard_normal(F) * 0.3),
            "scale_ffn": bf(0.1 * (1.0 + 0.1 * np.random.standard_normal(1)))}


def core(o, xn, W_O_words, W_O_scales, scale_attn, ffn1_w_words, ffn1_w_scales, ffn1_b, scale_ffn):
    p = (mxq(f64(o), 3, "e4m3") @ unpack4(W_O_words, W_O_scales)) * f64(scale_attn)
    y = np.maximum(f64(xn) + p, 0.0)
    u = (mxq(y, 3, "e4m3") @ unpack4(ffn1_w_words, ffn1_w_scales)) + f64(ffn1_b)
    return np.maximum(u * f64(scale_ffn), 0.0)


def e4m3fn_bytes(y):
    return np.clip(np.asarray(y, np.float64), -448.0, 448.0).astype(np.float32).astype(ml_dtypes.float8_e4m3fn).view(np.uint8)


def e4m3fn_values(b):
    return np.asarray(b, np.uint8).view(ml_dtypes.float8_e4m3fn).astype(np.float64)


def setup_inputs():
    d = draw0()
    x0 = np.asarray(d['o']).astype(np.float64)
    s = (np.max(np.abs(x0), axis=(0, 1, 2), keepdims=True) / 448.0).astype(np.float32)
    out = {}
    for k, v in d.items():
        if k == 'o':
            out['o_bytes'] = e4m3fn_bytes(x0 / s.astype(np.float64))
            out['o_scale'] = s
        else:
            out[k] = v
    return out


def reference(o_bytes, o_scale, xn, W_O_words, W_O_scales, scale_attn, ffn1_w_words, ffn1_w_scales, ffn1_b, scale_ffn):
    return core(e4m3fn_values(o_bytes) * o_scale.astype(np.float64), xn, W_O_words, W_O_scales, scale_attn, ffn1_w_words, ffn1_w_scales, ffn1_b, scale_ffn)

@@ -1,0 +1,301 @@
+from contextlib import ExitStack
+
+import concourse.mybir as mybir
+from concourse.masks import make_identity
+
+F32 = mybir.dt.float32
+BF16 = mybir.dt.bfloat16
+U32 = mybir.dt.uint32
+I32 = mybir.dt.int32
+U8 = mybir.dt.uint8
+FP8 = mybir.dt.float8_e4m3fn
+FP8X4 = mybir.dt.float8_e4m3fn_x4
+FP4X4 = mybir.dt.float4_e2m1fn_x4
+ALU = mybir.AluOpType
+ACT = mybir.ActivationFunctionType
+
+T, K, C, F = 1024, 512, 512, 2048
+P = 128
+G = 4
+FA = 1536
+NFB = (F - FA) // P
+
+FLOPS = 2 * T * K * C + 2 * T * C * F
+
+
+def tile_transformerconvblock_pb_w4_kernel(
+    tc, o_bytes, o_scale, xn, W_O_words, W_O_scales, scale_attn, ffn1_w_words, ffn1_w_scales, ffn1_b, scale_ffn, out
+):
+    nc = tc.nc
+    o_v = o_bytes.rearrange("b h w k -> (b h w) k").rearrange("(g p j) k -> p g j k", p=P, j=2)
+    xn_v = xn.rearrange("b h w k -> (b h w) k").rearrange("(g p j) k -> p g j k", p=P, j=2)
+    out_v = out.rearrange("b h w k -> (b h w) k").rearrange("(g p j) k -> g j p k", p=P, j=2)
+
+    with ExitStack() as ctx:
+        keep = ctx.enter_context(tc.tile_pool(name="keep", bufs=1))
+        work = ctx.enter_context(tc.tile_pool(name="work", bufs=2))
+        hpool = ctx.enter_context(tc.tile_pool(name="hpool", bufs=8))
+        psum = ctx.enter_context(tc.psum_pool(name="psum", bufs=1))
+        ctx.enter_context(tc.manual_schedule())
+
+        ob8 = keep.tile([P, G, 2, K], U8, align_bytes=64, name="ob8")
+        xnt = keep.tile([P, G, 2, C], BF16, align_bytes=64, name="xnt")
+        osc = keep.tile([P, 4], F32, align_bytes=64, name="osc")
+        wo = keep.tile([P, 2 * C], U8, align_bytes=64, name="wo")
+        wo_sc = keep.tile([P, C], U8, align_bytes=64, name="wo_sc")
+        w1 = keep.tile([P, 2 * F], U8, align_bytes=64, name="w1")
+        w1_sc = keep.tile([P, F], U8, align_bytes=64, name="w1_sc")
+        sa = keep.tile([P, 1], BF16, align_bytes=64, name="sa")
+        sfb = keep.tile([P, 1], BF16, align_bytes=64, name="sfb")
+        sf = keep.tile([P, 1], F32, align_bytes=64, name="sf")
+        brow = keep.tile([P, P], BF16, align_bytes=64, name="brow")
+        bcol = keep.tile([P, 16], F32, align_bytes=64, name="bcol")
+        bb = keep.tile([P, FA], BF16, align_bytes=64, name="bb")
+        identb = keep.tile([P, P], BF16, align_bytes=64, name="identb")
+        identf = keep.tile([P, P], F32, align_bytes=64, name="identf")
+        warm = keep.tile([P, 1], F32, align_bytes=64, name="warm")
+
+        nc.vector.memset(wo_sc[:].bitcast(I32), 0)
+        nc.vector.memset(w1_sc[:].bitcast(I32), 0)
+        nc.vector.memset(brow[:], 0.0)
+        nc.vector.memset(warm[:], 0.0)
+        make_identity(nc, identb[:])
+        nc.sync.dma_start(out=ob8[:, 0], in_=o_v[:, 0])
+        nc.sync.dma_start(out=wo[:], in_=W_O_words[0])
+        nc.scalar.dma_start(out=osc[:], in_=o_scale.rearrange("a b c (p t) -> p (a b c t)", t=4))
+        nc.scalar.dma_start(out=sa[:], in_=scale_attn.partition_broadcast(P))
+        nc.scalar.dma_start(out=brow[0:16, :], in_=ffn1_b.rearrange("(c q) -> c q", q=P))
+        nc.scalar.dma_start(out=sfb[:], in_=scale_ffn.partition_broadcast(P))
+        for q in range(4):
+            nc.sync.dma_start(out=wo_sc[32 * q : 32 * q + 4, :].bitcast(I32), in_=W_O_scales[0, 4 * q : 4 * q + 4, :].bitcast(I32))
+        nc.sync.dma_start(out=xnt[:, 0], in_=xn_v[:, 0])
+        nc.sync.dma_start(out=ob8[:, 1:4], in_=o_v[:, 1:4])
+        nc.sync.dma_start(out=w1[:], in_=ffn1_w_words[0])
+        for q in range(4):
+            nc.sync.dma_start(out=w1_sc[32 * q : 32 * q + 4, :].bitcast(I32), in_=ffn1_w_scales[0, 4 * q : 4 * q + 4, :].bitcast(I32))
+        for g in range(1, G):
+            nc.sync.dma_start(out=xnt[:, g], in_=xn_v[:, g])
+        nc.scalar.activation(warm[:], warm[:], ACT.Relu)
+
+        obs, ogs, ocs, oss, ys, ygs, ycs, yss, trs, ps = {}, {}, {}, {}, {}, {}, {}, {}, {}, {}
+        hs = {}
+        for g in range(G):
+            obs[g] = keep.tile([P, 2, K], BF16, align_bytes=64, name="ob%d" % g)
+            ogs[g] = keep.tile([P, 2, P, 4], BF16, align_bytes=64, name="og%d" % g)
+            ocs[g] = keep.tile([P, 2 * P], U32, align_bytes=64, name="oc%d" % g)
+            oss[g] = keep.tile([P, 2 * P], U8, align_bytes=64, name="os%d" % g)
+            ys[g] = keep.tile([P, 2, C], BF16, align_bytes=64, name="y%d" % g)
+            ygs[g] = keep.tile([P, 2, P, 4], BF16, align_bytes=64, name="yg%d" % g)
+            ycs[g] = keep.tile([P, 2 * P], U32, align_bytes=64, name="yc%d" % g)
+            yss[g] = keep.tile([P, 2 * P], U8, align_bytes=64, name="ysc%d" % g)
+
+        def cast(g, eng, js=(0, 1)):
+            for j in js:
+                src = ob8[:, g, j, :].bitcast(FP8)
+                if eng == "S":
+                    nc.scalar.copy(out=obs[g][:, j, :], in_=src)
+                else:
+                    nc.vector.tensor_copy(out=obs[g][:, j, :], in_=src)
+
+        def tr(src, js=(0, 1)):
+            t_ps = psum.tile([P, 2, 4, P], BF16, tag="tr", bufs=2, name="t_ps")
+            v = src[:].rearrange("p j (m t) -> p j t m", t=4)
+            for j in js:
+                for t in range(4):
+                    nc.tensor.transpose(t_ps[:, j, t, :], v[:, j, t, :], identb[:])
+            return t_ps
+
+        def span(js):
+            return slice(js[0], js[-1] + 1)
+
+        def tr_o(g, js=(0, 1)):
+            trs[("o", g, js)] = tr(obs[g], js)
+
+        def mul_o(g, js=(0, 1)):
+            s = span(js)
+            nc.vector.tensor_tensor(
+                out=ogs[g][:, s],
+                in0=trs[("o", g, js)][:, s].rearrange("p j t r -> p j r t"),
+                in1=osc[:].unsqueeze(1).unsqueeze(1).to_broadcast([P, len(js), P, 4]),
+                op=ALU.mult,
+            )
+
+        def q_o(g, js=(0, 1)):
+            s = slice(js[0] * P, (js[-1] + 1) * P)
+            nc.vector.quantize_mx(out=ocs[g][:, s].bitcast(FP8X4), scales=oss[g][:, s], in_=ogs[g][:, span(js)].rearrange("p j r t -> p (j r t)"))
+
+        def mm1(g, j):
+            p = psum.tile([P, C], F32, tag="p", bufs=1, name="p_ps")
+            ps[(g, j)] = p
+            s = slice(j * P, (j + 1) * P)
+            nc.tensor.matmul_mx(p[:], lhsT=ocs[g][:, s].bitcast(FP8X4), lhsT_scale=oss[g][:, s], rhs=wo[:].bitcast(FP4X4), rhs_scale=wo_sc[:], start=True, stop=True)
+
+        def add(g, j):
+            nc.vector.scalar_tensor_tensor(out=ys[g][:, j, :], in0=ps[(g, j)][:], scalar=sa[:], in1=xnt[:, g, j, :], op0=ALU.mult, op1=ALU.add)
+
+        def tr_y(g, js=(0, 1)):
+            trs[("y", g, js)] = tr(ys[g], js)
+
+        def relu_y(g, js=(0, 1)):
+            s = span(js)
+            nc.scalar.activation(ygs[g][:, s], trs[("y", g, js)][:, s].rearrange("p j t r -> p j r t"), ACT.Relu)
+
+        def q_y(g, js=(0, 1)):
+            s = slice(js[0] * P, (js[-1] + 1) * P)
+            nc.vector.quantize_mx(out=ycs[g][:, s].bitcast(FP8X4), scales=yss[g][:, s], in_=ygs[g][:, span(js)].rearrange("p j r t -> p (j r t)"))
+
+        us = {}
+
+        def h_tile(g, j, half):
+            if (g, j, half) not in hs:
+                h = hpool.tile([P, 1024], F32, align_bytes=64, name="h")
+                hs[(g, j, half)] = h
+            return hs[(g, j, half)]
+
+        def mm_a(g, j, f):
+            u = psum.tile([P, 512], F32, tag="u", bufs=3, name="u_ps")
+            us[(g, j, f)] = u
+            s = slice(j * P, (j + 1) * P)
+            nc.tensor.matmul_mx(u[:], lhsT=ycs[g][:, s].bitcast(FP8X4), lhsT_scale=yss[g][:, s], rhs=w1[:, 1024 * f : 1024 * (f + 1)].bitcast(FP4X4), rhs_scale=w1_sc[:, 512 * f : 512 * (f + 1)], start=True, stop=True)
+
+        def ev_a(g, j, f):
+            h = h_tile(g, j, f // 2)[:, 512 * (f % 2) : 512 * (f % 2) + 512]
+            nc.vector.tensor_tensor(out=h, in0=us[(g, j, f)][:], in1=bb[:, 512 * f : 512 * (f + 1)], op=ALU.add)
+
+        def relu_a(g, j, f, eng):
+            h = h_tile(g, j, f // 2)[:, 512 * (f % 2) : 512 * (f % 2) + 512]
+            if eng == "S":
+                nc.scalar.activation(h, h, ACT.Relu, scale=sf[:])
+            elif eng == "G":
+                nc.gpsimd.tensor_scalar(out=h, in0=h, scalar1=sf[:], scalar2=0.0, op0=ALU.mult, op1=ALU.max)
+            else:
+                nc.vector.tensor_scalar(out=h, in0=h, scalar1=sf[:], scalar2=0.0, op0=ALU.mult, op1=ALU.max)
+
+        def store(g, j, half):
+            nc.sync.dma_start(out=out_v[g, j][:, 1024 * half : 1024 * (half + 1)], in_=hs[(g, j, half)][:])
+
+        c1s, c1ps, c2ps = {}, {}, {}
+
+        def mm_c(g):
+            for fb in range(NFB):
+                if fb % 2 == 0:
+                    c1 = psum.tile([P, 2, 2 * P], F32, tag="c", bufs=2, name="c1_ps")
+                    c1ps[(g, fb // 2)] = c1
+                f0 = FA + P * fb
+                nc.tensor.matmul_mx(c1ps[(g, fb // 2)][:, fb % 2, :], lhsT=w1[:, 2 * f0 : 2 * (f0 + P)].bitcast(FP4X4), lhsT_scale=w1_sc[:, f0 : f0 + P], rhs=ycs[g][:].bitcast(FP8X4), rhs_scale=yss[g][:], start=True, stop=True)
+
+        def ev_c1(g):
+            c1_sb = work.tile([P, NFB, 2 * P], F32, align_bytes=64, name="c1_sb")
+            c1s[g] = c1_sb
+            for fb in range(NFB):
+                nc.scalar.activation(c1_sb[:, fb, :], c1ps[(g, fb // 2)][:, fb % 2, :], ACT.Relu, bias=bcol[:, FA // P + fb : FA // P + fb + 1], scale=sf[:])
+
+        def tr_c(g):
+            for j in range(2):
+                c2 = psum.tile([P, NFB, P], F32, tag="c", bufs=2, name="c2_ps")
+                c2ps[(g, j)] = c2
+                for fb in range(NFB):
+                    nc.tensor.transpose(c2[:, fb, :], c1s[g][:, fb, j * P : (j + 1) * P], identf[:])
+
+        def ev_c2(g, j):
+            h = h_tile(g, j, 1)[:, 512:1024]
+            nc.scalar.copy(out=h, in_=c2ps[(g, j)][:].rearrange("p f r -> p (f r)"))
+
+        nc.vector.tensor_copy(out=identf[:], in_=identb[:])
+        cast(0, "S", (0,))
+        cast(0, "V", (1,))
+        tr_o(0, (0,))
+        tr_o(0, (1,))
+        mul_o(0, (0,))
+        mul_o(0, (1,))
+        q_o(0, (0,))
+        q_o(0, (1,))
+        mm1(0, 0)
+        cast(1, "S")
+        nc.vector.tensor_copy(out=sf[:], in_=sfb[:])
+        bt = psum.tile([P, P], BF16, tag="tr", bufs=2, name="bt_ps")
+        nc.tensor.transpose(bt[:], brow[:], identb[:])
+        tr_o(1)
+        add(0, 0)
+        mm1(0, 1)
+        nc.vector.tensor_scalar(out=bcol[:], in0=bt[:, 0:16], scalar1=sf[:], scalar2=None, op0=ALU.mult)
+        add(0, 1)
+        tr_y(0, (0,))
+        relu_y(0, (0,))
+        mul_o(1)
+        tr_y(0, (1,))
+        relu_y(0, (1,))
+        for f in range(FA // 512):
+            u = psum.tile([P, 512], F32, tag="u", bufs=3, name="bb_ps")
+            for c in range(4):
+                m = 4 * f + c
+                nc.tensor.matmul(u[:, c * P : (c + 1) * P], lhsT=identb[:, m : m + 1].to_broadcast([P, P]), rhs=brow[:], start=True, stop=True)
+            nc.scalar.copy(out=bb[:, 512 * f : 512 * (f + 1)], in_=u[:])
+        q_y(0, (0,))
+        q_o(1)
+        q_y(0, (1,))
+        mm1(1, 0)
+        cast(2, "S")
+
+        order = [(0, 0), (1, 0), (0, 1), (1, 1), (0, 2), (1, 2)]
+        for g in range(G):
+            n1 = g + 1 < G
+            n2 = g + 2 < G
+            n3 = g + 3 < G
+            r = ["G", "S", "G", "S", "G", "S"] if n1 else ["S", "V", "S", "V", "S", "V"]
+            pend = []
+
+            def a_mm(i):
+                mm_a(g, *order[i])
+
+            def a_ev(i):
+                ev_a(g, *order[i])
+                while pend:
+                    relu_a(g, *order[pend.pop()], "V")
+                if r[i] == "V":
+                    pend.append(i)
+                else:
+                    relu_a(g, *order[i], r[i])
+
+            a_mm(0)
+            if n1:
+                add(g + 1, 0)
+                mm1(g + 1, 1)
+            a_ev(0)
+            a_mm(1)
+            if n1:
+                add(g + 1, 1)
+            mm_c(g)
+            ev_c1(g)
+            a_ev(1)
+            if n2:
+                tr_o(g + 2)
+                mul_o(g + 2)
+            if n1:
+                tr_y(g + 1)
+                relu_y(g + 1)
+            a_mm(2)
+            a_ev(2)
+            a_mm(3)
+            a_ev(3)
+            store(g, 0, 0)
+            if n2:
+                q_o(g + 2)
+            tr_c(g)
+            ev_c2(g, 0)
+            ev_c2(g, 1)
+            if n3:
+                cast(g + 3, "S")
+            if n1:
+                q_y(g + 1)
+            a_mm(4)
+            a_ev(4)
+            store(g, 1, 0)
+            a_mm(5)
+            a_ev(5)
+            while pend:
+                relu_a(g, *order[pend.pop()], "V")
+            store(g, 0, 1)
+            store(g, 1, 1)
+            if n2:
+                mm1(g + 2, 0)

@@ -19,6 +19,7 @@ P = 128
 G = 4
 FA = 1536
 NFB = (F - FA) // P
+RELU = ["SSVSVS", "SSVSVS", "SSVSVS", "SVSVSV"]
 
 FLOPS = 2 * T * K * C + 2 * T * C * F
 
@@ -34,7 +35,7 @@ def tile_transformerconvblock_pb_w4_kernel(
     with ExitStack() as ctx:
         keep = ctx.enter_context(tc.tile_pool(name="keep", bufs=1))
         work = ctx.enter_context(tc.tile_pool(name="work", bufs=2))
-        hpool = ctx.enter_context(tc.tile_pool(name="hpool", bufs=8))
+        hpool = ctx.enter_context(tc.tile_pool(name="hpool", bufs=16))
         psum = ctx.enter_context(tc.psum_pool(name="psum", bufs=1))
         ctx.enter_context(tc.manual_schedule())
 
@@ -51,29 +52,32 @@ def tile_transformerconvblock_pb_w4_kernel(
         brow = keep.tile([P, P], BF16, align_bytes=64, name="brow")
         bcol = keep.tile([P, 16], F32, align_bytes=64, name="bcol")
         bb = keep.tile([P, FA], BF16, align_bytes=64, name="bb")
+        scb = keep.tile([P, K], F32, align_bytes=64, name="scb")
         identb = keep.tile([P, P], BF16, align_bytes=64, name="identb")
         identf = keep.tile([P, P], F32, align_bytes=64, name="identf")
         warm = keep.tile([P, 1], F32, align_bytes=64, name="warm")
 
+        nc.vector.memset(brow[:].bitcast(I32), 0)
         nc.vector.memset(wo_sc[:].bitcast(I32), 0)
         nc.vector.memset(w1_sc[:].bitcast(I32), 0)
-        nc.vector.memset(brow[:], 0.0)
         nc.vector.memset(warm[:], 0.0)
+        nc.gpsimd.dma_start(out=osc[:], in_=o_scale.rearrange("a b c (p t) -> p (a b c t)", t=4))
         make_identity(nc, identb[:])
         nc.sync.dma_start(out=ob8[:, 0], in_=o_v[:, 0])
-        nc.sync.dma_start(out=wo[:], in_=W_O_words[0])
-        nc.scalar.dma_start(out=osc[:], in_=o_scale.rearrange("a b c (p t) -> p (a b c t)", t=4))
-        nc.scalar.dma_start(out=sa[:], in_=scale_attn.partition_broadcast(P))
         nc.scalar.dma_start(out=brow[0:16, :], in_=ffn1_b.rearrange("(c q) -> c q", q=P))
-        nc.scalar.dma_start(out=sfb[:], in_=scale_ffn.partition_broadcast(P))
+        nc.sync.dma_start(out=wo[:], in_=W_O_words[0])
         for q in range(4):
             nc.sync.dma_start(out=wo_sc[32 * q : 32 * q + 4, :].bitcast(I32), in_=W_O_scales[0, 4 * q : 4 * q + 4, :].bitcast(I32))
+        nc.gpsimd.dma_start(out=sa[:], in_=scale_attn.partition_broadcast(P))
+        nc.gpsimd.dma_start(out=sfb[:], in_=scale_ffn.partition_broadcast(P))
         nc.sync.dma_start(out=xnt[:, 0], in_=xn_v[:, 0])
-        nc.sync.dma_start(out=ob8[:, 1:4], in_=o_v[:, 1:4])
+        nc.sync.dma_start(out=ob8[:, 1:3], in_=o_v[:, 1:3])
         nc.sync.dma_start(out=w1[:], in_=ffn1_w_words[0])
         for q in range(4):
             nc.sync.dma_start(out=w1_sc[32 * q : 32 * q + 4, :].bitcast(I32), in_=ffn1_w_scales[0, 4 * q : 4 * q + 4, :].bitcast(I32))
-        for g in range(1, G):
+        nc.sync.dma_start(out=xnt[:, 1], in_=xn_v[:, 1])
+        nc.sync.dma_start(out=ob8[:, 3], in_=o_v[:, 3])
+        for g in range(2, G):
             nc.sync.dma_start(out=xnt[:, g], in_=xn_v[:, g])
         nc.scalar.activation(warm[:], warm[:], ACT.Relu)
 
@@ -120,12 +124,26 @@ def tile_transformerconvblock_pb_w4_kernel(
                 op=ALU.mult,
             )
 
+        def mul_n(g, j):
+            nc.vector.tensor_tensor(out=obs[g][:, j, :], in0=ob8[:, g, j, :].bitcast(FP8), in1=scb[:], op=ALU.mult)
+
+        def tr_n(g):
+            t_ps = psum.tile([P, 2, 2, P], F32, tag="tr", bufs=2, name="tn_ps")
+            v = obs[g][:].bitcast(F32).rearrange("p j (m u) -> p j u m", u=2)
+            for j in range(2):
+                for u in range(2):
+                    nc.tensor.transpose(t_ps[:, j, u, :], v[:, j, u, :], identf[:])
+            trs[("n", g)] = t_ps
+
+        def ev_n(g):
+            nc.scalar.copy(out=ogs[g][:].rearrange("p j r t -> p j (r t)").bitcast(F32).rearrange("p j (r u) -> p j r u", u=2), in_=trs[("n", g)][:].rearrange("p j u r -> p j r u"))
+
         def q_o(g, js=(0, 1)):
             s = slice(js[0] * P, (js[-1] + 1) * P)
             nc.vector.quantize_mx(out=ocs[g][:, s].bitcast(FP8X4), scales=oss[g][:, s], in_=ogs[g][:, span(js)].rearrange("p j r t -> p (j r t)"))
 
         def mm1(g, j):
-            p = psum.tile([P, C], F32, tag="p", bufs=1, name="p_ps")
+            p = psum.tile([P, C], F32, tag="u", bufs=4, name="p_ps")
             ps[(g, j)] = p
             s = slice(j * P, (j + 1) * P)
             nc.tensor.matmul_mx(p[:], lhsT=ocs[g][:, s].bitcast(FP8X4), lhsT_scale=oss[g][:, s], rhs=wo[:].bitcast(FP4X4), rhs_scale=wo_sc[:], start=True, stop=True)
@@ -136,8 +154,11 @@ def tile_transformerconvblock_pb_w4_kernel(
         def tr_y(g, js=(0, 1)):
             trs[("y", g, js)] = tr(ys[g], js)
 
-        def relu_y(g, js=(0, 1)):
+        def relu_y(g, js=(0, 1), eng="S"):
             s = span(js)
+            if eng == "V":
+                nc.vector.tensor_scalar(out=ygs[g][:, s], in0=trs[("y", g, js)][:, s].rearrange("p j t r -> p j r t"), scalar1=0.0, scalar2=None, op0=ALU.max)
+                return
             nc.scalar.activation(ygs[g][:, s], trs[("y", g, js)][:, s].rearrange("p j t r -> p j r t"), ACT.Relu)
 
         def q_y(g, js=(0, 1)):
@@ -146,33 +167,34 @@ def tile_transformerconvblock_pb_w4_kernel(
 
         us = {}
 
-        def h_tile(g, j, half):
-            if (g, j, half) not in hs:
-                h = hpool.tile([P, 1024], F32, align_bytes=64, name="h")
-                hs[(g, j, half)] = h
-            return hs[(g, j, half)]
+        def h_tile(g, j, f):
+            if (g, j, f) not in hs:
+                h = hpool.tile([P, 512], F32, align_bytes=64, name="h")
+                hs[(g, j, f)] = h
+            return hs[(g, j, f)][:]
 
         def mm_a(g, j, f):
-            u = psum.tile([P, 512], F32, tag="u", bufs=3, name="u_ps")
+            u = psum.tile([P, 512], F32, tag="u", bufs=4, name="u_ps")
             us[(g, j, f)] = u
             s = slice(j * P, (j + 1) * P)
             nc.tensor.matmul_mx(u[:], lhsT=ycs[g][:, s].bitcast(FP8X4), lhsT_scale=yss[g][:, s], rhs=w1[:, 1024 * f : 1024 * (f + 1)].bitcast(FP4X4), rhs_scale=w1_sc[:, 512 * f : 512 * (f + 1)], start=True, stop=True)
 
         def ev_a(g, j, f):
-            h = h_tile(g, j, f // 2)[:, 512 * (f % 2) : 512 * (f % 2) + 512]
+            h = h_tile(g, j, f)
             nc.vector.tensor_tensor(out=h, in0=us[(g, j, f)][:], in1=bb[:, 512 * f : 512 * (f + 1)], op=ALU.add)
 
         def relu_a(g, j, f, eng):
-            h = h_tile(g, j, f // 2)[:, 512 * (f % 2) : 512 * (f % 2) + 512]
+            h = h_tile(g, j, f)
             if eng == "S":
                 nc.scalar.activation(h, h, ACT.Relu, scale=sf[:])
             elif eng == "G":
                 nc.gpsimd.tensor_scalar(out=h, in0=h, scalar1=sf[:], scalar2=0.0, op0=ALU.mult, op1=ALU.max)
             else:
                 nc.vector.tensor_scalar(out=h, in0=h, scalar1=sf[:], scalar2=0.0, op0=ALU.mult, op1=ALU.max)
+            finished(g, j, f)
 
-        def store(g, j, half):
-            nc.sync.dma_start(out=out_v[g, j][:, 1024 * half : 1024 * (half + 1)], in_=hs[(g, j, half)][:])
+        def finished(g, j, f):
+            nc.sync.dma_start(out=out_v[g, j][:, 512 * f : 512 * (f + 1)], in_=hs[(g, j, f)][:])
 
         c1s, c1ps, c2ps = {}, {}, {}
 
@@ -198,104 +220,140 @@ def tile_transformerconvblock_pb_w4_kernel(
                     nc.tensor.transpose(c2[:, fb, :], c1s[g][:, fb, j * P : (j + 1) * P], identf[:])
 
         def ev_c2(g, j):
-            h = h_tile(g, j, 1)[:, 512:1024]
+            h = h_tile(g, j, 3)
             nc.scalar.copy(out=h, in_=c2ps[(g, j)][:].rearrange("p f r -> p (f r)"))
+            finished(g, j, 3)
 
-        nc.vector.tensor_copy(out=identf[:], in_=identb[:])
-        cast(0, "S", (0,))
-        cast(0, "V", (1,))
-        tr_o(0, (0,))
-        tr_o(0, (1,))
-        mul_o(0, (0,))
-        mul_o(0, (1,))
-        q_o(0, (0,))
-        q_o(0, (1,))
-        mm1(0, 0)
-        cast(1, "S")
-        nc.vector.tensor_copy(out=sf[:], in_=sfb[:])
-        bt = psum.tile([P, P], BF16, tag="tr", bufs=2, name="bt_ps")
-        nc.tensor.transpose(bt[:], brow[:], identb[:])
-        tr_o(1)
-        add(0, 0)
-        mm1(0, 1)
-        nc.vector.tensor_scalar(out=bcol[:], in0=bt[:, 0:16], scalar1=sf[:], scalar2=None, op0=ALU.mult)
-        add(0, 1)
-        tr_y(0, (0,))
-        relu_y(0, (0,))
-        mul_o(1)
-        tr_y(0, (1,))
-        relu_y(0, (1,))
-        for f in range(FA // 512):
-            u = psum.tile([P, 512], F32, tag="u", bufs=3, name="bb_ps")
+        def bias_rows(f):
+            u = psum.tile([P, 512], F32, tag="u", bufs=4, name="bb_ps")
             for c in range(4):
                 m = 4 * f + c
                 nc.tensor.matmul(u[:, c * P : (c + 1) * P], lhsT=identb[:, m : m + 1].to_broadcast([P, P]), rhs=brow[:], start=True, stop=True)
             nc.scalar.copy(out=bb[:, 512 * f : 512 * (f + 1)], in_=u[:])
-        q_y(0, (0,))
-        q_o(1)
-        q_y(0, (1,))
-        mm1(1, 0)
-        cast(2, "S")
 
-        order = [(0, 0), (1, 0), (0, 1), (1, 1), (0, 2), (1, 2)]
+        nc.vector.tensor_copy(out=identf[:], in_=identb[:])
+        cast(0, "V", (0,))
+        cast(0, "S", (1,))
+        tr_o(0, (0,))
+        tr_o(0, (1,))
+        mul_o(0, (0,))
+        sc_ps = psum.tile([P, 4, P], F32, tag="u", bufs=4, name="sc_ps")
+        for t in range(4):
+            nc.tensor.transpose(sc_ps[:, t, :], osc[:, t : t + 1].to_broadcast([P, P]), identf[:])
+        nc.scalar.copy(out=scb[:].rearrange("a (p t) -> a p t", t=4), in_=sc_ps[:].rearrange("a t p -> a p t"))
+        q_o(0, (0,))
+        mul_o(0, (1,))
+        for f in range(3):
+            bias_rows(f)
+        mm1(0, 0)
+        add(0, 0)
+        q_o(0, (1,))
+        mm1(0, 1)
+        mul_n(1, 0)
+        add(0, 1)
+        tr_y(0, (0,))
+        relu_y(0, (0,))
+        bt = psum.tile([P, P], BF16, tag="c", bufs=2, name="bt_ps")
+        nc.tensor.transpose(bt[:], brow[:], identb[:])
+        tr_y(0, (1,))
+        q_y(0, (0,))
+        relu_y(0, (1,))
+        mul_n(1, 1)
+        nc.vector.tensor_copy(out=sf[:], in_=sfb[:])
+        nc.vector.tensor_scalar(out=bcol[:], in0=bt[:, 0:16], scalar1=sf[:], scalar2=None, op0=ALU.mult)
+
+        order = [(0, 0), (0, 1), (0, 2), (1, 0), (1, 1), (1, 2)]
         for g in range(G):
             n1 = g + 1 < G
             n2 = g + 2 < G
-            n3 = g + 3 < G
-            r = ["G", "S", "G", "S", "G", "S"] if n1 else ["S", "V", "S", "V", "S", "V"]
+            r = RELU[g]
             pend = []
 
             def a_mm(i):
                 mm_a(g, *order[i])
 
-            def a_ev(i):
-                ev_a(g, *order[i])
+            def flush():
                 while pend:
                     relu_a(g, *order[pend.pop()], "V")
+
+            def a_ev(i):
+                ev_a(g, *order[i])
+                flush()
                 if r[i] == "V":
                     pend.append(i)
                 else:
                     relu_a(g, *order[i], r[i])
 
+            if g == 0:
+                a_mm(0)
+                tr_n(1)
+                a_mm(1)
+                ev_n(1)
+                a_ev(0)
+                q_y(0, (1,))
+                a_mm(2)
+                a_ev(1)
+                q_o(1)
+                mm_c(0)
+                ev_c1(0)
+                mm1(1, 0)
+                a_ev(2)
+                a_mm(3)
+                add(1, 0)
+                mm1(1, 1)
+                mul_n(2, 0)
+                a_ev(3)
+                add(1, 1)
+                tr_y(1)
+                relu_y(1)
+                a_mm(4)
+                tr_c(0)
+                ev_c2(0, 0)
+                mul_n(2, 1)
+                a_ev(4)
+                tr_n(2)
+                ev_n(2)
+                a_mm(5)
+                q_y(1)
+                a_ev(5)
+                flush()
+                ev_c2(0, 1)
+                q_o(2)
+                continue
             a_mm(0)
-            if n1:
-                add(g + 1, 0)
-                mm1(g + 1, 1)
             a_ev(0)
-            a_mm(1)
             if n1:
+                mm1(g + 1, 0)
+                add(g + 1, 0)
+            a_mm(1)
+            a_ev(1)
+            if n1:
+                mm1(g + 1, 1)
                 add(g + 1, 1)
             mm_c(g)
             ev_c1(g)
-            a_ev(1)
-            if n2:
-                tr_o(g + 2)
-                mul_o(g + 2)
+            a_mm(2)
+            a_ev(2)
             if n1:
                 tr_y(g + 1)
                 relu_y(g + 1)
-            a_mm(2)
-            a_ev(2)
+            if n2:
+                mul_n(g + 2, 0)
+                mul_n(g + 2, 1)
             a_mm(3)
             a_ev(3)
-            store(g, 0, 0)
-            if n2:
-                q_o(g + 2)
+            a_mm(4)
             tr_c(g)
+            if n2:
+                tr_n(g + 2)
+                ev_n(g + 2)
             ev_c2(g, 0)
-            ev_c2(g, 1)
-            if n3:
-                cast(g + 3, "S")
+            a_ev(4)
             if n1:
                 q_y(g + 1)
-            a_mm(4)
-            a_ev(4)
-            store(g, 1, 0)
+            ev_c2(g, 1)
             a_mm(5)
             a_ev(5)
-            while pend:
-                relu_a(g, *order[pend.pop()], "V")
-            store(g, 0, 1)
-            store(g, 1, 1)
+            flush()
             if n2:
-                mm1(g + 2, 0)
+                q_o(g + 2)

@@ -19,7 +19,6 @@ P = 128
 G = 4
 FA = 1536
 NFB = (F - FA) // P
-RELU = ["SSVSVS", "SSVSVS", "SSVSVS", "SVSVSV"]
 
 FLOPS = 2 * T * K * C + 2 * T * C * F
 
@@ -57,28 +56,26 @@ def tile_transformerconvblock_pb_w4_kernel(
         identf = keep.tile([P, P], F32, align_bytes=64, name="identf")
         warm = keep.tile([P, 1], F32, align_bytes=64, name="warm")
 
-        nc.vector.memset(brow[:].bitcast(I32), 0)
         nc.vector.memset(wo_sc[:].bitcast(I32), 0)
+        nc.vector.memset(brow[:].bitcast(I32), 0)
         nc.vector.memset(w1_sc[:].bitcast(I32), 0)
         nc.vector.memset(warm[:], 0.0)
-        nc.gpsimd.dma_start(out=osc[:], in_=o_scale.rearrange("a b c (p t) -> p (a b c t)", t=4))
         make_identity(nc, identb[:])
         nc.sync.dma_start(out=ob8[:, 0], in_=o_v[:, 0])
+        nc.scalar.dma_start(out=osc[:], in_=o_scale.rearrange("a b c (p t) -> p (a b c t)", t=4))
         nc.scalar.dma_start(out=brow[0:16, :], in_=ffn1_b.rearrange("(c q) -> c q", q=P))
         nc.sync.dma_start(out=wo[:], in_=W_O_words[0])
         for q in range(4):
             nc.sync.dma_start(out=wo_sc[32 * q : 32 * q + 4, :].bitcast(I32), in_=W_O_scales[0, 4 * q : 4 * q + 4, :].bitcast(I32))
-        nc.gpsimd.dma_start(out=sa[:], in_=scale_attn.partition_broadcast(P))
-        nc.gpsimd.dma_start(out=sfb[:], in_=scale_ffn.partition_broadcast(P))
         nc.sync.dma_start(out=xnt[:, 0], in_=xn_v[:, 0])
-        nc.sync.dma_start(out=ob8[:, 1:3], in_=o_v[:, 1:3])
-        nc.sync.dma_start(out=w1[:], in_=ffn1_w_words[0])
+        nc.sync.dma_start(out=ob8[:, 1:4], in_=o_v[:, 1:4])
         for q in range(4):
             nc.sync.dma_start(out=w1_sc[32 * q : 32 * q + 4, :].bitcast(I32), in_=ffn1_w_scales[0, 4 * q : 4 * q + 4, :].bitcast(I32))
+        nc.sync.dma_start(out=w1[:], in_=ffn1_w_words[0])
         nc.sync.dma_start(out=xnt[:, 1], in_=xn_v[:, 1])
-        nc.sync.dma_start(out=ob8[:, 3], in_=o_v[:, 3])
-        for g in range(2, G):
-            nc.sync.dma_start(out=xnt[:, g], in_=xn_v[:, g])
+        nc.sync.dma_start(out=xnt[:, 2:4], in_=xn_v[:, 2:4])
+        nc.gpsimd.dma_start(out=sa[:], in_=scale_attn.partition_broadcast(P))
+        nc.gpsimd.dma_start(out=sfb[:], in_=scale_ffn.partition_broadcast(P))
         nc.scalar.activation(warm[:], warm[:], ACT.Relu)
 
         obs, ogs, ocs, oss, ys, ygs, ycs, yss, trs, ps = {}, {}, {}, {}, {}, {}, {}, {}, {}, {}
@@ -198,26 +195,26 @@ def tile_transformerconvblock_pb_w4_kernel(
 
         c1s, c1ps, c2ps = {}, {}, {}
 
-        def mm_c(g):
-            for fb in range(NFB):
-                if fb % 2 == 0:
-                    c1 = psum.tile([P, 2, 2 * P], F32, tag="c", bufs=2, name="c1_ps")
-                    c1ps[(g, fb // 2)] = c1
-                f0 = FA + P * fb
-                nc.tensor.matmul_mx(c1ps[(g, fb // 2)][:, fb % 2, :], lhsT=w1[:, 2 * f0 : 2 * (f0 + P)].bitcast(FP4X4), lhsT_scale=w1_sc[:, f0 : f0 + P], rhs=ycs[g][:].bitcast(FP8X4), rhs_scale=yss[g][:], start=True, stop=True)
+        def mm_c(g, h):
+            c1 = psum.tile([P, 2, 2 * P], F32, tag="c", bufs=2, name="c1_ps")
+            c1ps[(g, h)] = c1
+            for i in range(2):
+                f0 = FA + P * (2 * h + i)
+                nc.tensor.matmul_mx(c1[:, i, :], lhsT=w1[:, 2 * f0 : 2 * (f0 + P)].bitcast(FP4X4), lhsT_scale=w1_sc[:, f0 : f0 + P], rhs=ycs[g][:].bitcast(FP8X4), rhs_scale=yss[g][:], start=True, stop=True)
 
-        def ev_c1(g):
-            c1_sb = work.tile([P, NFB, 2 * P], F32, align_bytes=64, name="c1_sb")
-            c1s[g] = c1_sb
-            for fb in range(NFB):
-                nc.scalar.activation(c1_sb[:, fb, :], c1ps[(g, fb // 2)][:, fb % 2, :], ACT.Relu, bias=bcol[:, FA // P + fb : FA // P + fb + 1], scale=sf[:])
+        def ev_c1(g, h):
+            if g not in c1s:
+                c1_sb = work.tile([P, NFB, 2 * P], F32, align_bytes=64, name="c1_sb")
+                c1s[g] = c1_sb
+            for i in range(2):
+                fb = 2 * h + i
+                nc.scalar.activation(c1s[g][:, fb, :], c1ps[(g, h)][:, i, :], ACT.Relu, bias=bcol[:, FA // P + fb : FA // P + fb + 1], scale=sf[:])
 
-        def tr_c(g):
-            for j in range(2):
-                c2 = psum.tile([P, NFB, P], F32, tag="c", bufs=2, name="c2_ps")
-                c2ps[(g, j)] = c2
-                for fb in range(NFB):
-                    nc.tensor.transpose(c2[:, fb, :], c1s[g][:, fb, j * P : (j + 1) * P], identf[:])
+        def tr_c(g, j):
+            c2 = psum.tile([P, NFB, P], F32, tag="c", bufs=2, name="c2_ps")
+            c2ps[(g, j)] = c2
+            for fb in range(NFB):
+                nc.tensor.transpose(c2[:, fb, :], c1s[g][:, fb, j * P : (j + 1) * P], identf[:])
 
         def ev_c2(g, j):
             h = h_tile(g, j, 3)
@@ -243,117 +240,87 @@ def tile_transformerconvblock_pb_w4_kernel(
         nc.scalar.copy(out=scb[:].rearrange("a (p t) -> a p t", t=4), in_=sc_ps[:].rearrange("a t p -> a p t"))
         q_o(0, (0,))
         mul_o(0, (1,))
-        for f in range(3):
-            bias_rows(f)
+        bias_rows(0)
         mm1(0, 0)
-        add(0, 0)
         q_o(0, (1,))
+        add(0, 0)
+        bias_rows(1)
+        bias_rows(2)
         mm1(0, 1)
         mul_n(1, 0)
-        add(0, 1)
         tr_y(0, (0,))
         relu_y(0, (0,))
+        add(0, 1)
+        mul_n(1, 1)
+        tr_y(0, (1,))
+        relu_y(0, (1,))
+        mul_n(2, 0)
+        q_y(0, (0,))
         bt = psum.tile([P, P], BF16, tag="c", bufs=2, name="bt_ps")
         nc.tensor.transpose(bt[:], brow[:], identb[:])
-        tr_y(0, (1,))
-        q_y(0, (0,))
-        relu_y(0, (1,))
-        mul_n(1, 1)
         nc.vector.tensor_copy(out=sf[:], in_=sfb[:])
         nc.vector.tensor_scalar(out=bcol[:], in0=bt[:, 0:16], scalar1=sf[:], scalar2=None, op0=ALU.mult)
+        mul_n(2, 1)
+        q_y(0, (1,))
 
-        order = [(0, 0), (0, 1), (0, 2), (1, 0), (1, 1), (1, 2)]
-        for g in range(G):
+        for g in range(-1, G):
+            here = g >= 0
             n1 = g + 1 < G
             n2 = g + 2 < G
-            r = RELU[g]
-            pend = []
-
-            def a_mm(i):
-                mm_a(g, *order[i])
-
-            def flush():
-                while pend:
-                    relu_a(g, *order[pend.pop()], "V")
-
-            def a_ev(i):
-                ev_a(g, *order[i])
-                flush()
-                if r[i] == "V":
-                    pend.append(i)
-                else:
-                    relu_a(g, *order[i], r[i])
-
-            if g == 0:
-                a_mm(0)
-                tr_n(1)
-                a_mm(1)
-                ev_n(1)
-                a_ev(0)
-                q_y(0, (1,))
-                a_mm(2)
-                a_ev(1)
-                q_o(1)
-                mm_c(0)
-                ev_c1(0)
-                mm1(1, 0)
-                a_ev(2)
-                a_mm(3)
-                add(1, 0)
-                mm1(1, 1)
-                mul_n(2, 0)
-                a_ev(3)
-                add(1, 1)
-                tr_y(1)
-                relu_y(1)
-                a_mm(4)
-                tr_c(0)
-                ev_c2(0, 0)
-                mul_n(2, 1)
-                a_ev(4)
-                tr_n(2)
-                ev_n(2)
-                a_mm(5)
-                q_y(1)
-                a_ev(5)
-                flush()
-                ev_c2(0, 1)
-                q_o(2)
-                continue
-            a_mm(0)
-            a_ev(0)
-            if n1:
-                mm1(g + 1, 0)
-                add(g + 1, 0)
-            a_mm(1)
-            a_ev(1)
-            if n1:
-                mm1(g + 1, 1)
-                add(g + 1, 1)
-            mm_c(g)
-            ev_c1(g)
-            a_mm(2)
-            a_ev(2)
-            if n1:
-                tr_y(g + 1)
-                relu_y(g + 1)
-            if n2:
+            n3 = g + 3 < G and g >= 0
+            if here:
+                mm_c(g, 0)
+                ev_c1(g, 0)
+            if g >= 1:
+                relu_a(g - 1, 0, 2, "S")
+            if here:
+                ev_a(g, 1, 0)
+                relu_a(g, 1, 0, "S")
+            if n2 and g >= 1:
                 mul_n(g + 2, 0)
-                mul_n(g + 2, 1)
-            a_mm(3)
-            a_ev(3)
-            a_mm(4)
-            tr_c(g)
+            if here:
+                mm_a(g, 0, 1)
+                ev_a(g, 0, 1)
+                mm_a(g, 1, 1)
+                ev_a(g, 1, 1)
+                if n1:
+                    tr_y(g + 1)
+                    relu_y(g + 1)
+                relu_a(g, 0, 1, "V")
+            if n3:
+                mul_n(g + 3, 1)
             if n2:
                 tr_n(g + 2)
                 ev_n(g + 2)
-            ev_c2(g, 0)
-            a_ev(4)
-            if n1:
-                q_y(g + 1)
-            ev_c2(g, 1)
-            a_mm(5)
-            a_ev(5)
-            flush()
+            if here:
+                mm_a(g, 1, 2)
+                ev_a(g, 1, 2)
+                if n1:
+                    q_y(g + 1)
             if n2:
                 q_o(g + 2)
+            if here:
+                tr_c(g, 0)
+                ev_c2(g, 0)
+                tr_c(g, 1)
+                ev_c2(g, 1)
+                relu_a(g, 1, 1, "S")
+                mm_a(g, 0, 2)
+                ev_a(g, 0, 2)
+            if n1:
+                mm_a(g + 1, 0, 0)
+                ev_a(g + 1, 0, 0)
+                mm_c(g + 1, 1)
+                ev_c1(g + 1, 1)
+                relu_a(g + 1, 0, 0, "S" if g + 1 < G - 1 else "V")
+            if n2:
+                mm1(g + 2, 0)
+                add(g + 2, 0)
+                mm1(g + 2, 1)
+                add(g + 2, 1)
+            if here:
+                relu_a(g, 1, 2, "V")
+            if n1:
+                mm_a(g + 1, 1, 0)
+            else:
+                relu_a(g, 0, 2, "V")

@@ -54,11 +54,13 @@ def tile_transformerconvblock_pb_w4_kernel(
         scb = keep.tile([P, K], F32, align_bytes=64, name="scb")
         identb = keep.tile([P, P], BF16, align_bytes=64, name="identb")
         identf = keep.tile([P, P], F32, align_bytes=64, name="identf")
+        zero = keep.tile([P, 512], BF16, align_bytes=64, name="zero")
         warm = keep.tile([P, 1], F32, align_bytes=64, name="warm")
 
         nc.vector.memset(wo_sc[:].bitcast(I32), 0)
         nc.vector.memset(brow[:].bitcast(I32), 0)
         nc.vector.memset(w1_sc[:].bitcast(I32), 0)
+        nc.vector.memset(zero[:].bitcast(I32), 0)
         nc.vector.memset(warm[:], 0.0)
         make_identity(nc, identb[:])
         nc.sync.dma_start(out=ob8[:, 0], in_=o_v[:, 0])
@@ -98,42 +100,34 @@ def tile_transformerconvblock_pb_w4_kernel(
                 else:
                     nc.vector.tensor_copy(out=obs[g][:, j, :], in_=src)
 
-        def tr(src, js=(0, 1)):
-            t_ps = psum.tile([P, 2, 4, P], BF16, tag="tr", bufs=2, name="t_ps")
-            v = src[:].rearrange("p j (m t) -> p j t m", t=4)
-            for j in js:
-                for t in range(4):
-                    nc.tensor.transpose(t_ps[:, j, t, :], v[:, j, t, :], identb[:])
-            return t_ps
-
         def span(js):
             return slice(js[0], js[-1] + 1)
 
-        def tr_o(g, js=(0, 1)):
-            trs[("o", g, js)] = tr(obs[g], js)
+        def tr(kind, src, g, js=(0, 1)):
+            t_ps = psum.tile([P, 2, 2, P], F32, tag="tr", bufs=2, name="t_ps")
+            v = src[g][:].bitcast(F32).rearrange("p j (m u) -> p j u m", u=2)
+            for j in js:
+                for u in range(2):
+                    nc.tensor.transpose(t_ps[:, j, u, :], v[:, j, u, :], identf[:])
+            trs[(kind, g, js)] = t_ps
 
-        def mul_o(g, js=(0, 1)):
+        def ev(kind, dst, g, js=(0, 1)):
             s = span(js)
+            nc.scalar.copy(
+                out=dst[g][:, s].rearrange("p j r t -> p j (r t)").bitcast(F32).rearrange("p j (r u) -> p j r u", u=2),
+                in_=trs[(kind, g, js)][:, s].rearrange("p j u r -> p j r u"),
+            )
+
+        def mul_o(g, j):
             nc.vector.tensor_tensor(
-                out=ogs[g][:, s],
-                in0=trs[("o", g, js)][:, s].rearrange("p j t r -> p j r t"),
-                in1=osc[:].unsqueeze(1).unsqueeze(1).to_broadcast([P, len(js), P, 4]),
+                out=ogs[g][:, j].rearrange("p r (u e) -> p r u e", u=2),
+                in0=trs[("o", g, (j,))][:, j].rearrange("p u r -> p (u r)").bitcast(BF16).rearrange("p (u r e) -> p r u e", u=2, e=2),
+                in1=osc[:].rearrange("p (u e) -> p u e", u=2).unsqueeze(1).to_broadcast([P, P, 2, 2]),
                 op=ALU.mult,
             )
 
         def mul_n(g, j):
             nc.vector.tensor_tensor(out=obs[g][:, j, :], in0=ob8[:, g, j, :].bitcast(FP8), in1=scb[:], op=ALU.mult)
-
-        def tr_n(g):
-            t_ps = psum.tile([P, 2, 2, P], F32, tag="tr", bufs=2, name="tn_ps")
-            v = obs[g][:].bitcast(F32).rearrange("p j (m u) -> p j u m", u=2)
-            for j in range(2):
-                for u in range(2):
-                    nc.tensor.transpose(t_ps[:, j, u, :], v[:, j, u, :], identf[:])
-            trs[("n", g)] = t_ps
-
-        def ev_n(g):
-            nc.scalar.copy(out=ogs[g][:].rearrange("p j r t -> p j (r t)").bitcast(F32).rearrange("p j (r u) -> p j r u", u=2), in_=trs[("n", g)][:].rearrange("p j u r -> p j r u"))
 
         def q_o(g, js=(0, 1)):
             s = slice(js[0] * P, (js[-1] + 1) * P)
@@ -148,15 +142,8 @@ def tile_transformerconvblock_pb_w4_kernel(
         def add(g, j):
             nc.vector.scalar_tensor_tensor(out=ys[g][:, j, :], in0=ps[(g, j)][:], scalar=sa[:], in1=xnt[:, g, j, :], op0=ALU.mult, op1=ALU.add)
 
-        def tr_y(g, js=(0, 1)):
-            trs[("y", g, js)] = tr(ys[g], js)
-
-        def relu_y(g, js=(0, 1), eng="S"):
-            s = span(js)
-            if eng == "V":
-                nc.vector.tensor_scalar(out=ygs[g][:, s], in0=trs[("y", g, js)][:, s].rearrange("p j t r -> p j r t"), scalar1=0.0, scalar2=None, op0=ALU.max)
-                return
-            nc.scalar.activation(ygs[g][:, s], trs[("y", g, js)][:, s].rearrange("p j t r -> p j r t"), ACT.Relu)
+        def relu_y(g, j):
+            nc.vector.tensor_scalar(out=ys[g][:, j, :], in0=ys[g][:, j, :], scalar1=0.0, scalar2=None, op0=ALU.max)
 
         def q_y(g, js=(0, 1)):
             s = slice(js[0] * P, (js[-1] + 1) * P)
@@ -221,106 +208,119 @@ def tile_transformerconvblock_pb_w4_kernel(
             nc.scalar.copy(out=h, in_=c2ps[(g, j)][:].rearrange("p f r -> p (f r)"))
             finished(g, j, 3)
 
-        def bias_rows(f):
+        bias_ps = {}
+
+        def bias_mm(f):
             u = psum.tile([P, 512], F32, tag="u", bufs=4, name="bb_ps")
             for c in range(4):
                 m = 4 * f + c
                 nc.tensor.matmul(u[:, c * P : (c + 1) * P], lhsT=identb[:, m : m + 1].to_broadcast([P, P]), rhs=brow[:], start=True, stop=True)
-            nc.scalar.copy(out=bb[:, 512 * f : 512 * (f + 1)], in_=u[:])
+            bias_ps[f] = u
+
+        def bias_ev(f):
+            nc.scalar.copy(out=bb[:, 512 * f : 512 * (f + 1)], in_=bias_ps[f][:])
+
+        def bias_rows(f):
+            bias_mm(f)
+            bias_ev(f)
 
         nc.vector.tensor_copy(out=identf[:], in_=identb[:])
+        for i in range(4):
+            dummy = psum.tile([P, 512], F32, tag="c", bufs=2, name="dummy_ps")
+            nc.tensor.matmul(dummy[:], lhsT=identb[:], rhs=zero[:], start=True, stop=True)
         cast(0, "V", (0,))
         cast(0, "S", (1,))
-        tr_o(0, (0,))
-        tr_o(0, (1,))
-        mul_o(0, (0,))
         sc_ps = psum.tile([P, 4, P], F32, tag="u", bufs=4, name="sc_ps")
         for t in range(4):
             nc.tensor.transpose(sc_ps[:, t, :], osc[:, t : t + 1].to_broadcast([P, P]), identf[:])
         nc.scalar.copy(out=scb[:].rearrange("a (p t) -> a p t", t=4), in_=sc_ps[:].rearrange("a t p -> a p t"))
+        tr("o", obs, 0, (0,))
+        tr("o", obs, 0, (1,))
+        mul_o(0, 0)
+        mul_o(0, 1)
+        bias_rows(2)
         q_o(0, (0,))
-        mul_o(0, (1,))
-        bias_rows(0)
         mm1(0, 0)
         q_o(0, (1,))
-        add(0, 0)
-        bias_rows(1)
-        bias_rows(2)
+        bias_mm(1)
         mm1(0, 1)
-        mul_n(1, 0)
-        tr_y(0, (0,))
-        relu_y(0, (0,))
-        add(0, 1)
         mul_n(1, 1)
-        tr_y(0, (1,))
-        relu_y(0, (1,))
-        mul_n(2, 0)
-        q_y(0, (0,))
+        mul_n(1, 0)
+        add(0, 1)
+        add(0, 0)
         bt = psum.tile([P, P], BF16, tag="c", bufs=2, name="bt_ps")
         nc.tensor.transpose(bt[:], brow[:], identb[:])
-        nc.vector.tensor_copy(out=sf[:], in_=sfb[:])
-        nc.vector.tensor_scalar(out=bcol[:], in0=bt[:, 0:16], scalar1=sf[:], scalar2=None, op0=ALU.mult)
+        tr("o", obs, 1)
+        ev("o", ogs, 1)
+        bias_ev(1)
+        bias_mm(0)
+        relu_y(0, 1)
+        relu_y(0, 0)
+        tr("y", ys, 0, (1,))
+        ev("y", ygs, 0, (1,))
+        tr("y", ys, 0, (0,))
+        ev("y", ygs, 0, (0,))
+        bias_ev(0)
+        mul_n(2, 0)
+        q_o(1)
         mul_n(2, 1)
         q_y(0, (1,))
+        nc.vector.tensor_copy(out=sf[:], in_=sfb[:])
+        nc.vector.tensor_scalar(out=bcol[:], in0=bt[:, 0:16], scalar1=sf[:], scalar2=None, op0=ALU.mult)
+        q_y(0, (0,))
+        mm1(1, 1)
+        mm1(1, 0)
 
-        for g in range(-1, G):
-            here = g >= 0
-            n1 = g + 1 < G
-            n2 = g + 2 < G
-            n3 = g + 3 < G and g >= 0
-            if here:
-                mm_c(g, 0)
-                ev_c1(g, 0)
-            if g >= 1:
-                relu_a(g - 1, 0, 2, "S")
-            if here:
-                ev_a(g, 1, 0)
-                relu_a(g, 1, 0, "S")
-            if n2 and g >= 1:
-                mul_n(g + 2, 0)
-            if here:
-                mm_a(g, 0, 1)
-                ev_a(g, 0, 1)
-                mm_a(g, 1, 1)
-                ev_a(g, 1, 1)
-                if n1:
-                    tr_y(g + 1)
-                    relu_y(g + 1)
-                relu_a(g, 0, 1, "V")
-            if n3:
-                mul_n(g + 3, 1)
-            if n2:
-                tr_n(g + 2)
-                ev_n(g + 2)
-            if here:
-                mm_a(g, 1, 2)
-                ev_a(g, 1, 2)
-                if n1:
-                    q_y(g + 1)
-            if n2:
-                q_o(g + 2)
-            if here:
-                tr_c(g, 0)
-                ev_c2(g, 0)
-                tr_c(g, 1)
-                ev_c2(g, 1)
-                relu_a(g, 1, 1, "S")
-                mm_a(g, 0, 2)
-                ev_a(g, 0, 2)
-            if n1:
-                mm_a(g + 1, 0, 0)
-                ev_a(g + 1, 0, 0)
-                mm_c(g + 1, 1)
-                ev_c1(g + 1, 1)
-                relu_a(g + 1, 0, 0, "S" if g + 1 < G - 1 else "V")
-            if n2:
-                mm1(g + 2, 0)
-                add(g + 2, 0)
-                mm1(g + 2, 1)
-                add(g + 2, 1)
-            if here:
-                relu_a(g, 1, 2, "V")
-            if n1:
-                mm_a(g + 1, 1, 0)
-            else:
-                relu_a(g, 0, 2, "V")
+        def step(f, g, *rest):
+            if 0 <= g < G:
+                f(g, *rest)
+
+        for g in range(G + 1):
+            if g > 0:
+                step(mul_n, g + 2, 0)
+            step(ev_a, g - 1, 1, 1)
+            step(mm_a, g - 1, 1, 2)
+            if g + 2 < G:
+                tr("o", obs, g + 2)
+            if g > 0:
+                step(q_y, g)
+            step(ev_a, g - 1, 0, 1)
+            step(mm_a, g, 0, 0)
+            step(mm_c, g, 1)
+            step(add, g + 1, 1)
+            step(add, g + 1, 0)
+            step(mm_a, g - 1, 0, 2)
+            step(mm_c, g, 0)
+            step(ev_a, g - 1, 1, 2)
+            if g < G:
+                step(relu_a, g - 1, 1, 0, "S")
+            step(relu_a, g - 1, 1, 1, "S")
+            step(relu_a, g - 1, 0, 1, "S")
+            if g + 2 < G:
+                ev("o", ogs, g + 2)
+            step(ev_c1, g, 1)
+            step(ev_c1, g, 0)
+            step(relu_y, g + 1, 0)
+            step(mul_n, g + 3, 1)
+            step(relu_y, g + 1, 1)
+            step(mm_a, g, 1, 0)
+            step(mm_a, g, 1, 1)
+            step(ev_a, g, 0, 0)
+            step(relu_a, g, 0, 0, "S")
+            if g + 1 < G:
+                tr("y", ys, g + 1)
+                ev("y", ygs, g + 1)
+            step(ev_a, g - 1, 0, 2)
+            step(relu_a, g - 1, 1, 2, "V")
+            step(q_o, g + 2)
+            step(relu_a, g - 1, 0, 2, "V")
+            step(tr_c, g, 0)
+            step(ev_c2, g, 0)
+            step(tr_c, g, 1)
+            step(ev_c2, g, 1)
+            step(mm_a, g, 0, 1)
+            step(mm1, g + 2, 1)
+            step(ev_a, g, 1, 0)
+            step(mm1, g + 2, 0)
+            if g == G - 1:
+                step(relu_a, g, 1, 0, "V")

from contextlib import ExitStack

import concourse.mybir as mybir
from concourse.masks import make_identity

F32 = mybir.dt.float32
BF16 = mybir.dt.bfloat16
U32 = mybir.dt.uint32
I32 = mybir.dt.int32
U8 = mybir.dt.uint8
FP8 = mybir.dt.float8_e4m3fn
FP8X4 = mybir.dt.float8_e4m3fn_x4
FP4X4 = mybir.dt.float4_e2m1fn_x4
ALU = mybir.AluOpType
ACT = mybir.ActivationFunctionType

T, K, C, F = 1024, 512, 512, 2048
P = 128
G = 4
FA = 1536
NFB = (F - FA) // P

FLOPS = 2 * T * K * C + 2 * T * C * F


def tile_transformerconvblock_pb_w4_kernel(
    tc, o_bytes, o_scale, xn, W_O_words, W_O_scales, scale_attn, ffn1_w_words, ffn1_w_scales, ffn1_b, scale_ffn, out
):
    nc = tc.nc
    o_v = o_bytes.rearrange("b h w k -> (b h w) k").rearrange("(g p j) k -> p g j k", p=P, j=2)
    xn_v = xn.rearrange("b h w k -> (b h w) k").rearrange("(g p j) k -> p g j k", p=P, j=2)
    out_v = out.rearrange("b h w k -> (b h w) k").rearrange("(g p j) k -> g j p k", p=P, j=2)

    with ExitStack() as ctx:
        keep = ctx.enter_context(tc.tile_pool(name="keep", bufs=1))
        work = ctx.enter_context(tc.tile_pool(name="work", bufs=2))
        hpool = ctx.enter_context(tc.tile_pool(name="hpool", bufs=16))
        psum = ctx.enter_context(tc.psum_pool(name="psum", bufs=1))
        ctx.enter_context(tc.manual_schedule())

        ob8 = keep.tile([P, G, 2, K], U8, align_bytes=64, name="ob8")
        xnt = keep.tile([P, G, 2, C], BF16, align_bytes=64, name="xnt")
        osc = keep.tile([P, 4], F32, align_bytes=64, name="osc")
        wo = keep.tile([P, 2 * C], U8, align_bytes=64, name="wo")
        wo_sc = keep.tile([P, C], U8, align_bytes=64, name="wo_sc")
        w1 = keep.tile([P, 2 * F], U8, align_bytes=64, name="w1")
        w1_sc = keep.tile([P, F], U8, align_bytes=64, name="w1_sc")
        sa = keep.tile([P, 1], BF16, align_bytes=64, name="sa")
        sfb = keep.tile([P, 1], BF16, align_bytes=64, name="sfb")
        sf = keep.tile([P, 1], F32, align_bytes=64, name="sf")
        brow = keep.tile([P, P], BF16, align_bytes=64, name="brow")
        bcol = keep.tile([P, 16], F32, align_bytes=64, name="bcol")
        bb = keep.tile([P, FA], BF16, align_bytes=64, name="bb")
        scb = keep.tile([P, K], F32, align_bytes=64, name="scb")
        identb = keep.tile([P, P], BF16, align_bytes=64, name="identb")
        identf = keep.tile([P, P], F32, align_bytes=64, name="identf")
        zero = keep.tile([P, 512], BF16, align_bytes=64, name="zero")
        warm = keep.tile([P, 1], F32, align_bytes=64, name="warm")

        nc.vector.memset(wo_sc[:].bitcast(I32), 0)
        nc.vector.memset(brow[:].bitcast(I32), 0)
        nc.vector.memset(w1_sc[:].bitcast(I32), 0)
        nc.vector.memset(zero[:].bitcast(I32), 0)
        nc.vector.memset(warm[:], 0.0)
        make_identity(nc, identb[:])
        nc.sync.dma_start(out=ob8[:, 0], in_=o_v[:, 0])
        nc.scalar.dma_start(out=osc[:], in_=o_scale.rearrange("a b c (p t) -> p (a b c t)", t=4))
        nc.scalar.dma_start(out=brow[0:16, :], in_=ffn1_b.rearrange("(c q) -> c q", q=P))
        nc.sync.dma_start(out=wo[:], in_=W_O_words[0])
        for q in range(4):
            nc.sync.dma_start(out=wo_sc[32 * q : 32 * q + 4, :].bitcast(I32), in_=W_O_scales[0, 4 * q : 4 * q + 4, :].bitcast(I32))
        nc.sync.dma_start(out=xnt[:, 0], in_=xn_v[:, 0])
        nc.sync.dma_start(out=ob8[:, 1:4], in_=o_v[:, 1:4])
        for q in range(4):
            nc.sync.dma_start(out=w1_sc[32 * q : 32 * q + 4, :].bitcast(I32), in_=ffn1_w_scales[0, 4 * q : 4 * q + 4, :].bitcast(I32))
        nc.sync.dma_start(out=w1[:], in_=ffn1_w_words[0])
        nc.sync.dma_start(out=xnt[:, 1], in_=xn_v[:, 1])
        nc.sync.dma_start(out=xnt[:, 2:4], in_=xn_v[:, 2:4])
        nc.gpsimd.dma_start(out=sa[:], in_=scale_attn.partition_broadcast(P))
        nc.gpsimd.dma_start(out=sfb[:], in_=scale_ffn.partition_broadcast(P))
        nc.scalar.activation(warm[:], warm[:], ACT.Relu)

        obs, ogs, ocs, oss, ys, ygs, ycs, yss, trs, ps = {}, {}, {}, {}, {}, {}, {}, {}, {}, {}
        hs = {}
        for g in range(G):
            obs[g] = keep.tile([P, 2, K], BF16, align_bytes=64, name="ob%d" % g)
            ogs[g] = keep.tile([P, 2, P, 4], BF16, align_bytes=64, name="og%d" % g)
            ocs[g] = keep.tile([P, 2 * P], U32, align_bytes=64, name="oc%d" % g)
            oss[g] = keep.tile([P, 2 * P], U8, align_bytes=64, name="os%d" % g)
            ys[g] = keep.tile([P, 2, C], BF16, align_bytes=64, name="y%d" % g)
            ygs[g] = keep.tile([P, 2, P, 4], BF16, align_bytes=64, name="yg%d" % g)
            ycs[g] = keep.tile([P, 2 * P], U32, align_bytes=64, name="yc%d" % g)
            yss[g] = keep.tile([P, 2 * P], U8, align_bytes=64, name="ysc%d" % g)

        def cast(g, eng, js=(0, 1)):
            for j in js:
                src = ob8[:, g, j, :].bitcast(FP8)
                if eng == "S":
                    nc.scalar.copy(out=obs[g][:, j, :], in_=src)
                else:
                    nc.vector.tensor_copy(out=obs[g][:, j, :], in_=src)

        def span(js):
            return slice(js[0], js[-1] + 1)

        def tr(kind, src, g, js=(0, 1)):
            t_ps = psum.tile([P, 2, 2, P], F32, tag="tr", bufs=2, name="t_ps")
            v = src[g][:].bitcast(F32).rearrange("p j (m u) -> p j u m", u=2)
            for j in js:
                for u in range(2):
                    nc.tensor.transpose(t_ps[:, j, u, :], v[:, j, u, :], identf[:])
            trs[(kind, g, js)] = t_ps

        def ev(kind, dst, g, js=(0, 1)):
            s = span(js)
            nc.scalar.copy(
                out=dst[g][:, s].rearrange("p j r t -> p j (r t)").bitcast(F32).rearrange("p j (r u) -> p j r u", u=2),
                in_=trs[(kind, g, js)][:, s].rearrange("p j u r -> p j r u"),
            )

        def mul_o(g, j):
            nc.vector.tensor_tensor(
                out=ogs[g][:, j].rearrange("p r (u e) -> p r u e", u=2),
                in0=trs[("o", g, (j,))][:, j].rearrange("p u r -> p (u r)").bitcast(BF16).rearrange("p (u r e) -> p r u e", u=2, e=2),
                in1=osc[:].rearrange("p (u e) -> p u e", u=2).unsqueeze(1).to_broadcast([P, P, 2, 2]),
                op=ALU.mult,
            )

        def mul_n(g, j):
            nc.vector.tensor_tensor(out=obs[g][:, j, :], in0=ob8[:, g, j, :].bitcast(FP8), in1=scb[:], op=ALU.mult)

        def q_o(g, js=(0, 1)):
            s = slice(js[0] * P, (js[-1] + 1) * P)
            nc.vector.quantize_mx(out=ocs[g][:, s].bitcast(FP8X4), scales=oss[g][:, s], in_=ogs[g][:, span(js)].rearrange("p j r t -> p (j r t)"))

        def mm1(g, j):
            p = psum.tile([P, C], F32, tag="u", bufs=4, name="p_ps")
            ps[(g, j)] = p
            s = slice(j * P, (j + 1) * P)
            nc.tensor.matmul_mx(p[:], lhsT=ocs[g][:, s].bitcast(FP8X4), lhsT_scale=oss[g][:, s], rhs=wo[:].bitcast(FP4X4), rhs_scale=wo_sc[:], start=True, stop=True)

        def add(g, j):
            nc.vector.scalar_tensor_tensor(out=ys[g][:, j, :], in0=ps[(g, j)][:], scalar=sa[:], in1=xnt[:, g, j, :], op0=ALU.mult, op1=ALU.add)

        def relu_y(g, j):
            nc.vector.tensor_scalar(out=ys[g][:, j, :], in0=ys[g][:, j, :], scalar1=0.0, scalar2=None, op0=ALU.max)

        def q_y(g, js=(0, 1)):
            s = slice(js[0] * P, (js[-1] + 1) * P)
            nc.vector.quantize_mx(out=ycs[g][:, s].bitcast(FP8X4), scales=yss[g][:, s], in_=ygs[g][:, span(js)].rearrange("p j r t -> p (j r t)"))

        us = {}

        def h_tile(g, j, f):
            if (g, j, f) not in hs:
                h = hpool.tile([P, 512], F32, align_bytes=64, name="h")
                hs[(g, j, f)] = h
            return hs[(g, j, f)][:]

        def mm_a(g, j, f):
            u = psum.tile([P, 512], F32, tag="u", bufs=4, name="u_ps")
            us[(g, j, f)] = u
            s = slice(j * P, (j + 1) * P)
            nc.tensor.matmul_mx(u[:], lhsT=ycs[g][:, s].bitcast(FP8X4), lhsT_scale=yss[g][:, s], rhs=w1[:, 1024 * f : 1024 * (f + 1)].bitcast(FP4X4), rhs_scale=w1_sc[:, 512 * f : 512 * (f + 1)], start=True, stop=True)

        def ev_a(g, j, f):
            h = h_tile(g, j, f)
            nc.vector.tensor_tensor(out=h, in0=us[(g, j, f)][:], in1=bb[:, 512 * f : 512 * (f + 1)], op=ALU.add)

        def relu_a(g, j, f, eng):
            h = h_tile(g, j, f)
            if eng == "S":
                nc.scalar.activation(h, h, ACT.Relu, scale=sf[:])
            elif eng == "G":
                nc.gpsimd.tensor_scalar(out=h, in0=h, scalar1=sf[:], scalar2=0.0, op0=ALU.mult, op1=ALU.max)
            else:
                nc.vector.tensor_scalar(out=h, in0=h, scalar1=sf[:], scalar2=0.0, op0=ALU.mult, op1=ALU.max)
            finished(g, j, f)

        def finished(g, j, f):
            nc.sync.dma_start(out=out_v[g, j][:, 512 * f : 512 * (f + 1)], in_=hs[(g, j, f)][:])

        c1s, c1ps, c2ps = {}, {}, {}

        def mm_c(g, h):
            c1 = psum.tile([P, 2, 2 * P], F32, tag="c", bufs=2, name="c1_ps")
            c1ps[(g, h)] = c1
            for i in range(2):
                f0 = FA + P * (2 * h + i)
                nc.tensor.matmul_mx(c1[:, i, :], lhsT=w1[:, 2 * f0 : 2 * (f0 + P)].bitcast(FP4X4), lhsT_scale=w1_sc[:, f0 : f0 + P], rhs=ycs[g][:].bitcast(FP8X4), rhs_scale=yss[g][:], start=True, stop=True)

        def ev_c1(g, h):
            if g not in c1s:
                c1_sb = work.tile([P, NFB, 2 * P], F32, align_bytes=64, name="c1_sb")
                c1s[g] = c1_sb
            for i in range(2):
                fb = 2 * h + i
                nc.scalar.activation(c1s[g][:, fb, :], c1ps[(g, h)][:, i, :], ACT.Relu, bias=bcol[:, FA // P + fb : FA // P + fb + 1], scale=sf[:])

        def tr_c(g, j):
            c2 = psum.tile([P, NFB, P], F32, tag="c", bufs=2, name="c2_ps")
            c2ps[(g, j)] = c2
            for fb in range(NFB):
                nc.tensor.transpose(c2[:, fb, :], c1s[g][:, fb, j * P : (j + 1) * P], identf[:])

        def ev_c2(g, j):
            h = h_tile(g, j, 3)
            nc.scalar.copy(out=h, in_=c2ps[(g, j)][:].rearrange("p f r -> p (f r)"))
            finished(g, j, 3)

        bias_ps = {}

        def bias_mm(f):
            u = psum.tile([P, 512], F32, tag="u", bufs=4, name="bb_ps")
            for c in range(4):
                m = 4 * f + c
                nc.tensor.matmul(u[:, c * P : (c + 1) * P], lhsT=identb[:, m : m + 1].to_broadcast([P, P]), rhs=brow[:], start=True, stop=True)
            bias_ps[f] = u

        def bias_ev(f):
            nc.scalar.copy(out=bb[:, 512 * f : 512 * (f + 1)], in_=bias_ps[f][:])

        def bias_rows(f):
            bias_mm(f)
            bias_ev(f)

        nc.vector.tensor_copy(out=identf[:], in_=identb[:])
        for i in range(4):
            dummy = psum.tile([P, 512], F32, tag="c", bufs=2, name="dummy_ps")
            nc.tensor.matmul(dummy[:], lhsT=identb[:], rhs=zero[:], start=True, stop=True)
        cast(0, "V", (0,))
        cast(0, "S", (1,))
        sc_ps = psum.tile([P, 4, P], F32, tag="u", bufs=4, name="sc_ps")
        for t in range(4):
            nc.tensor.transpose(sc_ps[:, t, :], osc[:, t : t + 1].to_broadcast([P, P]), identf[:])
        nc.scalar.copy(out=scb[:].rearrange("a (p t) -> a p t", t=4), in_=sc_ps[:].rearrange("a t p -> a p t"))
        tr("o", obs, 0, (0,))
        tr("o", obs, 0, (1,))
        mul_o(0, 0)
        mul_o(0, 1)
        bias_rows(2)
        q_o(0, (0,))
        mm1(0, 0)
        q_o(0, (1,))
        bias_mm(1)
        mm1(0, 1)
        mul_n(1, 1)
        mul_n(1, 0)
        add(0, 1)
        add(0, 0)
        bt = psum.tile([P, P], BF16, tag="c", bufs=2, name="bt_ps")
        nc.tensor.transpose(bt[:], brow[:], identb[:])
        tr("o", obs, 1)
        ev("o", ogs, 1)
        bias_ev(1)
        bias_mm(0)
        relu_y(0, 1)
        relu_y(0, 0)
        tr("y", ys, 0, (1,))
        ev("y", ygs, 0, (1,))
        tr("y", ys, 0, (0,))
        ev("y", ygs, 0, (0,))
        bias_ev(0)
        mul_n(2, 0)
        q_o(1)
        mul_n(2, 1)
        q_y(0, (1,))
        nc.vector.tensor_copy(out=sf[:], in_=sfb[:])
        nc.vector.tensor_scalar(out=bcol[:], in0=bt[:, 0:16], scalar1=sf[:], scalar2=None, op0=ALU.mult)
        q_y(0, (0,))
        mm1(1, 1)
        mm1(1, 0)

        def step(f, g, *rest):
            if 0 <= g < G:
                f(g, *rest)

        for g in range(G + 1):
            if g > 0:
                step(mul_n, g + 2, 0)
            step(ev_a, g - 1, 1, 1)
            step(mm_a, g - 1, 1, 2)
            if g + 2 < G:
                tr("o", obs, g + 2)
            if g > 0:
                step(q_y, g)
            step(ev_a, g - 1, 0, 1)
            step(mm_a, g, 0, 0)
            step(mm_c, g, 1)
            step(add, g + 1, 1)
            step(add, g + 1, 0)
            step(mm_a, g - 1, 0, 2)
            step(mm_c, g, 0)
            step(ev_a, g - 1, 1, 2)
            if g < G:
                step(relu_a, g - 1, 1, 0, "S")
            step(relu_a, g - 1, 1, 1, "S")
            step(relu_a, g - 1, 0, 1, "S")
            if g + 2 < G:
                ev("o", ogs, g + 2)
            step(ev_c1, g, 1)
            step(ev_c1, g, 0)
            step(relu_y, g + 1, 0)
            step(mul_n, g + 3, 1)
            step(relu_y, g + 1, 1)
            step(mm_a, g, 1, 0)
            step(mm_a, g, 1, 1)
            step(ev_a, g, 0, 0)
            step(relu_a, g, 0, 0, "S")
            if g + 1 < G:
                tr("y", ys, g + 1)
                ev("y", ygs, g + 1)
            step(ev_a, g - 1, 0, 2)
            step(relu_a, g - 1, 1, 2, "V")
            step(q_o, g + 2)
            step(relu_a, g - 1, 0, 2, "V")
            step(tr_c, g, 0)
            step(ev_c2, g, 0)
            step(tr_c, g, 1)
            step(ev_c2, g, 1)
            step(mm_a, g, 0, 1)
            step(mm1, g + 2, 1)
            step(ev_a, g, 1, 0)
            step(mm1, g + 2, 0)
            if g == G - 1:
                step(relu_a, g, 1, 0, "V")
